import numpy as np
import ml_dtypes


def mxq(x, axis, fmt="e4m3"):
    dtype, down = {"e4m3": (ml_dtypes.float8_e4m3fn, 7), "e5m2": (ml_dtypes.float8_e5m2, 14)}[fmt]
    v = np.moveaxis(np.asarray(x, np.float32).astype(ml_dtypes.bfloat16).astype(np.float64), axis, -1)
    blocks = v.reshape(v.shape[:-1] + (-1, 32))
    amax = np.abs(blocks).max(-1, keepdims=True)
    byte = np.maximum(np.where(amax > 0, np.frexp(amax)[1] - 1 + 127, 0) - down, 1)
    scale = np.exp2(byte - 127.0)
    codes = (blocks / scale).astype(np.float32).astype(dtype).astype(np.float64)
    return np.moveaxis((codes * scale).reshape(v.shape), -1, axis)


WIDE = False


def mx_kscale(k):
    if not WIDE:
        return np.ones(k)
    levels = np.array([10, -10, 5, -5, 0])
    if k % 512:
        return np.exp2(np.random.permutation(np.resize(levels, k // 32))).repeat(32)
    a = np.empty((k // 512, 16))
    for p in range(k // 512):
        a[p, :8] = np.random.permutation(np.resize(levels, 8))
        for g in range(8):
            far = levels[np.abs(levels - a[p, g]) >= 10]
            a[p, g + 8] = far[np.random.randint(len(far))]
    return np.exp2(a.ravel()).repeat(32)


BF16 = ml_dtypes.bfloat16


def bf(x):
    return np.asarray(x, np.float32).astype(BF16)


def f64(x):
    return np.asarray(x).astype(np.float64)


B, T, D, H, KV, HD, QB = 1, 1024, 1024, 8, 1, 128, 512
HALF = HD // 2
THETA = 100000.0


def rope_tables():
    inv_freq = 1.0 / THETA ** (np.arange(0, HD, 2) / HD)
    ang = np.arange(T)[:, None] * inv_freq[None, :]
    return np.cos(ang), np.sin(ang)


def apply_rope(a, cos, sin):
    ar = a.reshape(a.shape[:-1] + (HALF, 2))
    a0, a1 = ar[..., 0], ar[..., 1]
    c = cos[None, :, None, :]
    s = sin[None, :, None, :]
    o0 = a0 * c - a1 * s
    o1 = a0 * s + a1 * c
    return np.stack([o0, o1], axis=-1).reshape(a.shape)


def setup_inputs():
    s = mx_kscale(D)
    cos, sin = rope_tables()
    return {"x": bf(np.random.standard_normal((B, T, D)) * s),
            "Wq": bf(np.random.standard_normal((D, H * HD)) * 1.5 / np.sqrt(D) / s[:, None]),
            "Wk": bf(np.random.standard_normal((D, KV * HD)) * 1.5 / np.sqrt(D) / s[:, None]),
            "Wv": bf(np.random.standard_normal((D, KV * HD)) / np.sqrt(D) / s[:, None]),
            "cos": bf(cos), "sin": bf(sin)}


def reference(x, Wq, Wk, Wv, cos, sin):
    xq = mxq(f64(x), 2, "e4m3")
    q = (xq @ mxq(f64(Wq), 0, "e4m3")).reshape(B, T, H, HD)
    k = (xq @ mxq(f64(Wk), 0, "e4m3")).reshape(B, T, KV, HD)
    v = (xq @ mxq(f64(Wv), 0, "e4m3")).reshape(B, T, KV, HD)
    q = apply_rope(q, f64(cos), f64(sin))
    k = apply_rope(k, f64(cos), f64(sin))
    return q, k[:, :, 0, :], v[:, :, 0, :]

@@ -1,0 +1,215 @@
+from contextlib import ExitStack
+
+from concourse import mybir
+from concourse.masks import make_identity
+
+F32 = mybir.dt.float32
+BF16 = mybir.dt.bfloat16
+U32 = mybir.dt.uint32
+U8 = mybir.dt.uint8
+FP8X4 = mybir.dt.float8_e4m3fn_x4
+MULT = mybir.AluOpType.mult
+ADD = mybir.AluOpType.add
+
+P = 128
+T = 1024
+D = 1024
+HEADS = 8
+HD = 128
+PAIRS = HD // 2
+PACK = 4
+K_PASS = P * PACK
+PASSES = D // K_PASS
+TILES = T // P
+BANK = 512
+CHUNK_HEADS = BANK // HD
+CHUNKS = HEADS // CHUNK_HEADS
+GROUP_TILES = BANK // HD
+
+FLOPS = 2 * T * D * (HEADS * HD + 2 * HD)
+
+
+def tile_attention_pa_kernel(tc, x, Wq, Wk, Wv, cos, sin, out_0, out_1, out_2):
+    nc = tc.nc
+
+    x_rows = x.flatten_outer_dims().rearrange("(p m) k -> p m k", m=TILES)
+    cos_rows = cos.rearrange("(p m) i -> p m i", m=TILES)
+    sin_rows = sin.rearrange("(p m) i -> p m i", m=TILES)
+    q_rows = out_0.rearrange("b t h d -> (b t) (h d)").rearrange("(p m) c -> p m c", m=TILES)
+    k_rows = out_1.flatten_outer_dims().rearrange("(p m) d -> p m d", m=TILES)
+    v_rows = out_2.flatten_outer_dims().rearrange("(p m) d -> p m d", m=TILES)
+
+    with ExitStack() as stack:
+        consts = stack.enter_context(tc.tile_pool(name="consts", bufs=1))
+        x_pool = stack.enter_context(tc.tile_pool(name="x_pool", bufs=TILES))
+        w_pool = stack.enter_context(tc.tile_pool(name="w_pool", bufs=CHUNKS * PASSES))
+        kv_pool = stack.enter_context(tc.tile_pool(name="kv_pool", bufs=1))
+        prod_pool = stack.enter_context(tc.tile_pool(name="prod_pool", bufs=4))
+        out_pool = stack.enter_context(tc.tile_pool(name="out_pool", bufs=6))
+        turn_psum = stack.enter_context(tc.psum_pool(name="turn_psum", bufs=2))
+        acc_psum = stack.enter_context(tc.psum_pool(name="acc_psum", bufs=6))
+
+        def load_weight_pass(raw, rows):
+            nc.sync.dma_start(out=raw[:], in_=rows.rearrange("(p t) c -> p t c", t=PACK))
+
+        planes = consts.tile([P, 3, TILES, PAIRS], BF16)
+        nc.scalar.dma_start(out=planes[:, 0], in_=sin_rows)
+        nc.scalar.dma_start(out=planes[:, 1], in_=cos_rows)
+
+        wq_raw = {}
+        x_raw = {}
+        for n in range(CHUNKS):
+            for g in range(PASSES):
+                wq_raw[n, g] = w_pool.tile([P, PACK, BANK], BF16, name="wq_raw")
+        for m in range(TILES):
+            x_raw[m] = x_pool.tile([P, D], BF16, name="x_raw")
+
+        def load_wq(n, g):
+            load_weight_pass(wq_raw[n, g], Wq[K_PASS * g : K_PASS * (g + 1), BANK * n : BANK * (n + 1)])
+
+        load_wq(0, 0)
+        nc.sync.dma_start(out=x_raw[0][:], in_=x_rows[:, 0, :])
+        load_wq(0, 1)
+        for m in range(1, TILES):
+            nc.sync.dma_start(out=x_raw[m][:], in_=x_rows[:, m, :])
+        kv_raw = kv_pool.tile([P, 2, PASSES, PACK, HD], BF16)
+        for w, weight in enumerate((Wk, Wv)):
+            nc.sync.dma_start(
+                out=kv_raw[:, w].rearrange("p g t c -> p g (t c)"),
+                in_=weight.rearrange("(g p t) c -> p g (t c)", p=P, t=PACK),
+            )
+        load_wq(1, 0)
+        load_wq(1, 1)
+
+        ident = consts.tile([P, P], F32)
+        make_identity(nc, ident[:])
+
+        nc.scalar.mul(out=planes[:, 2], in_=planes[:, 0], mul=-1.0)
+        table = consts.tile([P, TILES, 2, HD], F32)
+        for h in range(2):
+            nc.scalar.copy(
+                out=table[:, :, h, :].rearrange("p m (i j) -> p m i j", j=2),
+                in_=planes[:, 1 - h : 3 - h].rearrange("p j m i -> p m i j"),
+            )
+
+        def quantise_wq(n, copy_engine):
+            codes = consts.tile([P, PASSES, BANK], U32, name="wq_codes%d" % n, align_bytes=64)
+            scales = consts.tile([P, PASSES, BANK], U8, name="wq_scales%d" % n, align_bytes=64)
+            grouped = {}
+            for g in range(PASSES):
+                grouped[g] = w_pool.tile([P, BANK, PACK], BF16, name="wq_grouped", align_bytes=64)
+                copy_engine(out=grouped[g][:], in_=wq_raw[n, g][:].rearrange("p t c -> p c t"))
+            for g in range(PASSES):
+                nc.vector.quantize_mx(
+                    out=codes[:, g, :].bitcast(FP8X4),
+                    scales=scales[:, g, :],
+                    in_=grouped[g][:].rearrange("p c t -> p (c t)"),
+                )
+            return codes, scales
+
+        def quantise_kv():
+            codes = kv_pool.tile([P, 2, PASSES, HD], U32, name="kv_codes", align_bytes=64)
+            scales = kv_pool.tile([P, 2, PASSES, HD], U8, name="kv_scales", align_bytes=64)
+            grouped = kv_pool.tile([P, 2 * PASSES, HD, PACK], BF16, name="kv_grouped", align_bytes=64)
+            nc.scalar.copy(out=grouped[:], in_=kv_raw[:].rearrange("p w g t c -> p (w g) c t"))
+            nc.vector.quantize_mx(
+                out=codes[:].rearrange("p w g c -> p (w g c)").bitcast(FP8X4),
+                scales=scales[:].rearrange("p w g c -> p (w g c)"),
+                in_=grouped[:].rearrange("p a c t -> p (a c t)"),
+            )
+            return codes, scales
+
+        x_codes = {}
+        x_scales = {}
+
+        def quantise_x(m):
+            words = x_raw[m][:].bitcast(F32)
+            turned = turn_psum.tile([P, PASSES * 2, P], F32, name="turned")
+            for b in range(PASSES * 2):
+                first = 2 * P * (b // 2) + b % 2
+                nc.tensor.transpose(turned[:, b, :], words[:, first : 2 * P * (b // 2 + 1) : 2], ident[:])
+            grouped = x_pool.tile([P, PASSES * P * PACK], BF16, name="x_grouped", align_bytes=64)
+            nc.scalar.copy(
+                out=grouped[:].bitcast(F32).rearrange("p (g r u) -> p g r u", g=PASSES, u=2),
+                in_=turned[:].rearrange("p (g u) r -> p g r u", u=2),
+            )
+            x_codes[m] = x_pool.tile([P, PASSES, P], U32, name="x_codes", align_bytes=64)
+            x_scales[m] = x_pool.tile([P, PASSES, P], U8, name="x_scales", align_bytes=64)
+            nc.vector.quantize_mx(
+                out=x_codes[m][:].rearrange("p g r -> p (g r)").bitcast(FP8X4),
+                scales=x_scales[m][:].rearrange("p g r -> p (g r)"),
+                in_=grouped[:],
+            )
+
+        def project(acc, m, codes, scales):
+            for g in range(PASSES):
+                nc.tensor.matmul_mx(
+                    out=acc,
+                    lhsT=x_codes[m][:, g, :].bitcast(FP8X4),
+                    lhsT_scale=x_scales[m][:, g, :],
+                    rhs=codes[g].bitcast(FP8X4),
+                    rhs_scale=scales[g],
+                    start=(g == 0),
+                    stop=(g == PASSES - 1),
+                )
+
+        def rotate_and_store(acc, table_view, dest):
+            prod = prod_pool.tile([P, 2, BANK], F32, name="prod")
+            nc.vector.tensor_tensor(
+                out=prod[:].rearrange("p h (a d) -> p h a d", d=HD),
+                in0=acc.unsqueeze(1).to_broadcast([P, 2, BANK // HD, HD]),
+                in1=table_view,
+                op=MULT,
+            )
+            rot = out_pool.tile([P, BANK // 2, 2], F32, name="rot")
+            pairs = prod[:].rearrange("p h (n j) -> p n h j", j=2)
+            nc.gpsimd.tensor_tensor(out=rot[:], in0=pairs[:, :, :, 0], in1=pairs[:, :, :, 1], op=ADD)
+            nc.sync.dma_start(out=dest, in_=rot[:].rearrange("p n h -> p (n h)"))
+
+        def q_chunk(n, m, codes, scales):
+            acc = acc_psum.tile([P, CHUNK_HEADS, HD], F32, name="acc")
+            project(
+                acc[:].rearrange("p a d -> p (a d)"),
+                m,
+                [codes[:, g, :] for g in range(PASSES)],
+                [scales[:, g, :] for g in range(PASSES)],
+            )
+            rotate_and_store(
+                acc[:],
+                table[:, m].unsqueeze(2).to_broadcast([P, 2, CHUNK_HEADS, HD]),
+                q_rows[:, m, BANK * n : BANK * (n + 1)],
+            )
+
+        wq0_codes, wq0_scales = quantise_wq(0, nc.vector.tensor_copy)
+        quantise_x(0)
+        for m in range(TILES):
+            if m + 1 < TILES:
+                quantise_x(m + 1)
+            q_chunk(0, m, wq0_codes, wq0_scales)
+
+        kv_codes, kv_scales = quantise_kv()
+        wq1_codes, wq1_scales = quantise_wq(1, nc.scalar.copy)
+
+        for w in range(2):
+            for first in range(0, TILES, GROUP_TILES):
+                acc = acc_psum.tile([P, GROUP_TILES, HD], F32, name="acc")
+                for a in range(GROUP_TILES):
+                    project(
+                        acc[:, a, :],
+                        first + a,
+                        [kv_codes[:, w, g, :] for g in range(PASSES)],
+                        [kv_scales[:, w, g, :] for g in range(PASSES)],
+                    )
+                if w == 0:
+                    rotate_and_store(
+                        acc[:],
+                        table[:, first : first + GROUP_TILES].rearrange("p m h d -> p h m d"),
+                        k_rows[:, first : first + GROUP_TILES, :].rearrange("p m d -> p (m d)"),
+                    )
+                else:
+                    v_sb = out_pool.tile([P, GROUP_TILES, HD], F32, name="v_sb")
+                    nc.scalar.copy(out=v_sb[:], in_=acc[:])
+                    nc.sync.dma_start(out=v_rows[:, first : first + GROUP_TILES, :], in_=v_sb[:])
+
+        for m in range(TILES):
+            q_chunk(1, m, wq1_codes, wq1_scales)

@@ -22,8 +22,6 @@ K_PASS = P * PACK
 PASSES = D // K_PASS
 TILES = T // P
 BANK = 512
-CHUNK_HEADS = BANK // HD
-CHUNKS = HEADS // CHUNK_HEADS
 GROUP_TILES = BANK // HD
 
 FLOPS = 2 * T * D * (HEADS * HD + 2 * HD)
@@ -42,103 +40,113 @@ def tile_attention_pa_kernel(tc, x, Wq, Wk, Wv, cos, sin, out_0, out_1, out_2):
     with ExitStack() as stack:
         consts = stack.enter_context(tc.tile_pool(name="consts", bufs=1))
         x_pool = stack.enter_context(tc.tile_pool(name="x_pool", bufs=TILES))
-        w_pool = stack.enter_context(tc.tile_pool(name="w_pool", bufs=CHUNKS * PASSES))
-        kv_pool = stack.enter_context(tc.tile_pool(name="kv_pool", bufs=1))
         prod_pool = stack.enter_context(tc.tile_pool(name="prod_pool", bufs=4))
-        out_pool = stack.enter_context(tc.tile_pool(name="out_pool", bufs=6))
-        turn_psum = stack.enter_context(tc.psum_pool(name="turn_psum", bufs=2))
-        acc_psum = stack.enter_context(tc.psum_pool(name="acc_psum", bufs=6))
+        out_pool = stack.enter_context(tc.tile_pool(name="out_pool", bufs=8))
+        turn_psum = stack.enter_context(tc.psum_pool(name="turn_psum", bufs=3))
+        acc_psum = stack.enter_context(tc.psum_pool(name="acc_psum", bufs=5))
+        stack.enter_context(tc.manual_schedule())
 
-        def load_weight_pass(raw, rows):
-            nc.sync.dma_start(out=raw[:], in_=rows.rearrange("(p t) c -> p t c", t=PACK))
+        def weight_tiles(tag, width):
+            raw = consts.tile([P, PASSES, PACK, width], BF16, name=tag + "_raw")
+            grouped = consts.tile([P, PASSES, width, PACK], BF16, name=tag + "_grouped", align_bytes=64)
+            codes = consts.tile([P, PASSES, width], U32, name=tag + "_codes", align_bytes=64)
+            scales = consts.tile([P, PASSES, width], U8, name=tag + "_scales", align_bytes=64)
+            return raw, grouped, codes, scales
 
+        chunk_cols = [(0, 256), (256, 256), (512, 512)]
+        chunks = [weight_tiles("q%d" % n, width) for n, (first, width) in enumerate(chunk_cols)]
+        kv = weight_tiles("kv", 2 * HD)
+        x_raw = [x_pool.tile([P, D], BF16, name="x_raw") for m in range(TILES)]
         planes = consts.tile([P, 3, TILES, PAIRS], BF16)
-        nc.scalar.dma_start(out=planes[:, 0], in_=sin_rows)
-        nc.scalar.dma_start(out=planes[:, 1], in_=cos_rows)
+        table = consts.tile([P, 2, TILES, PAIRS, 2], BF16)
 
-        wq_raw = {}
-        x_raw = {}
-        for n in range(CHUNKS):
-            for g in range(PASSES):
-                wq_raw[n, g] = w_pool.tile([P, PACK, BANK], BF16, name="wq_raw")
-        for m in range(TILES):
-            x_raw[m] = x_pool.tile([P, D], BF16, name="x_raw")
-
-        def load_wq(n, g):
-            load_weight_pass(wq_raw[n, g], Wq[K_PASS * g : K_PASS * (g + 1), BANK * n : BANK * (n + 1)])
-
-        load_wq(0, 0)
-        nc.sync.dma_start(out=x_raw[0][:], in_=x_rows[:, 0, :])
-        load_wq(0, 1)
-        for m in range(1, TILES):
+        def load_x(m):
             nc.sync.dma_start(out=x_raw[m][:], in_=x_rows[:, m, :])
-        kv_raw = kv_pool.tile([P, 2, PASSES, PACK, HD], BF16)
-        for w, weight in enumerate((Wk, Wv)):
-            nc.sync.dma_start(
-                out=kv_raw[:, w].rearrange("p g t c -> p g (t c)"),
-                in_=weight.rearrange("(g p t) c -> p g (t c)", p=P, t=PACK),
-            )
-        load_wq(1, 0)
-        load_wq(1, 1)
+
+        def load_q(n):
+            first, width = chunk_cols[n]
+            for g in range(PASSES):
+                nc.sync.dma_start(
+                    out=chunks[n][0][:, g],
+                    in_=Wq[K_PASS * g : K_PASS * (g + 1), first : first + width].rearrange(
+                        "(p t) c -> p t c", t=PACK
+                    ),
+                )
+
+        def load_kv():
+            for w, weight in enumerate((Wk, Wv)):
+                for g in range(PASSES):
+                    nc.sync.dma_start(
+                        out=kv[0][:, g, :, HD * w : HD * (w + 1)],
+                        in_=weight[K_PASS * g : K_PASS * (g + 1), :].rearrange("(p t) c -> p t c", t=PACK),
+                    )
+
+        nc.scalar.dma_start(out=planes[:, 2], in_=sin_rows)
+        nc.scalar.dma_start(out=planes[:, 1], in_=cos_rows)
+        load_x(0)
+        load_q(0)
+        for m in range(1, TILES):
+            load_x(m)
+        load_q(1)
+        load_kv()
+        load_q(2)
 
         ident = consts.tile([P, P], F32)
         make_identity(nc, ident[:])
+        for first, last in ((0, 2), (2, TILES)):
 
-        nc.scalar.mul(out=planes[:, 2], in_=planes[:, 0], mul=-1.0)
-        table = consts.tile([P, TILES, 2, HD], F32)
-        for h in range(2):
-            nc.scalar.copy(
-                out=table[:, :, h, :].rearrange("p m (i j) -> p m i j", j=2),
-                in_=planes[:, 1 - h : 3 - h].rearrange("p j m i -> p m i j"),
-            )
+            def scaled(out, in_, factor):
+                nc.gpsimd.tensor_scalar(out=out, in0=in_, scalar1=factor, scalar2=0.0, op0=MULT, op1=ADD)
 
-        def quantise_wq(n, copy_engine):
-            codes = consts.tile([P, PASSES, BANK], U32, name="wq_codes%d" % n, align_bytes=64)
-            scales = consts.tile([P, PASSES, BANK], U8, name="wq_scales%d" % n, align_bytes=64)
-            grouped = {}
-            for g in range(PASSES):
-                grouped[g] = w_pool.tile([P, BANK, PACK], BF16, name="wq_grouped", align_bytes=64)
-                copy_engine(out=grouped[g][:], in_=wq_raw[n, g][:].rearrange("p t c -> p c t"))
-            for g in range(PASSES):
-                nc.vector.quantize_mx(
-                    out=codes[:, g, :].bitcast(FP8X4),
-                    scales=scales[:, g, :],
-                    in_=grouped[g][:].rearrange("p c t -> p (c t)"),
+            scaled(planes[:, 0, first:last], planes[:, 2, first:last], -1.0)
+            for e in range(2):
+                scaled(
+                    table[:, e, first:last], planes[:, 1 - e : 3 - e, first:last].rearrange("p h m i -> p m i h"), 1.0
                 )
-            return codes, scales
 
-        def quantise_kv():
-            codes = kv_pool.tile([P, 2, PASSES, HD], U32, name="kv_codes", align_bytes=64)
-            scales = kv_pool.tile([P, 2, PASSES, HD], U8, name="kv_scales", align_bytes=64)
-            grouped = kv_pool.tile([P, 2 * PASSES, HD, PACK], BF16, name="kv_grouped", align_bytes=64)
-            nc.scalar.copy(out=grouped[:], in_=kv_raw[:].rearrange("p w g t c -> p (w g) c t"))
-            nc.vector.quantize_mx(
-                out=codes[:].rearrange("p w g c -> p (w g c)").bitcast(FP8X4),
-                scales=scales[:].rearrange("p w g c -> p (w g c)"),
-                in_=grouped[:].rearrange("p a c t -> p (a c t)"),
+        def regroup(copy_engine, tiles, g, first, last):
+            raw, grouped = tiles[:2]
+            copy_engine(
+                out=grouped[:, g, first:last, :], in_=raw[:, g, :, first:last].rearrange("p t c -> p c t")
             )
-            return codes, scales
 
+        def quantise_weights(tiles, g):
+            raw, grouped, codes, scales = tiles
+            nc.vector.quantize_mx(
+                out=codes[:, g].bitcast(FP8X4),
+                scales=scales[:, g],
+                in_=grouped[:, g].rearrange("p c t -> p (c t)"),
+            )
+
+        x_grouped = {}
         x_codes = {}
         x_scales = {}
 
-        def quantise_x(m):
+        turned_x = {}
+
+        def turn_x(m):
             words = x_raw[m][:].bitcast(F32)
-            turned = turn_psum.tile([P, PASSES * 2, P], F32, name="turned")
-            for b in range(PASSES * 2):
-                first = 2 * P * (b // 2) + b % 2
-                nc.tensor.transpose(turned[:, b, :], words[:, first : 2 * P * (b // 2 + 1) : 2], ident[:])
-            grouped = x_pool.tile([P, PASSES * P * PACK], BF16, name="x_grouped", align_bytes=64)
+            turned = turn_psum.tile([P, PASSES, 2, P], F32, name="turned")
+            for g in range(PASSES):
+                for u in range(2):
+                    first = 2 * P * g
+                    nc.tensor.transpose(turned[:, g, u, :], words[:, first + u : first + 2 * P : 2], ident[:])
+            turned_x[m] = turned
+
+        def copy_x(m):
+            x_grouped[m] = x_pool.tile([P, PASSES * P * PACK], BF16, name="x_grouped", align_bytes=64)
             nc.scalar.copy(
-                out=grouped[:].bitcast(F32).rearrange("p (g r u) -> p g r u", g=PASSES, u=2),
-                in_=turned[:].rearrange("p (g u) r -> p g r u", u=2),
+                out=x_grouped[m][:].bitcast(F32).rearrange("p (g r u) -> p g r u", g=PASSES, u=2),
+                in_=turned_x[m][:].rearrange("p g u r -> p g r u"),
             )
+
+        def quantise_x(m):
             x_codes[m] = x_pool.tile([P, PASSES, P], U32, name="x_codes", align_bytes=64)
             x_scales[m] = x_pool.tile([P, PASSES, P], U8, name="x_scales", align_bytes=64)
             nc.vector.quantize_mx(
                 out=x_codes[m][:].rearrange("p g r -> p (g r)").bitcast(FP8X4),
                 scales=x_scales[m][:].rearrange("p g r -> p (g r)"),
-                in_=grouped[:],
+                in_=x_grouped[m][:],
             )
 
         def project(acc, m, codes, scales):
@@ -153,63 +161,140 @@ def tile_attention_pa_kernel(tc, x, Wq, Wk, Wv, cos, sin, out_0, out_1, out_2):
                     stop=(g == PASSES - 1),
                 )
 
-        def rotate_and_store(acc, table_view, dest):
-            prod = prod_pool.tile([P, 2, BANK], F32, name="prod")
+        def rotate_part(acc, tables, prod, first, width):
             nc.vector.tensor_tensor(
-                out=prod[:].rearrange("p h (a d) -> p h a d", d=HD),
-                in0=acc.unsqueeze(1).to_broadcast([P, 2, BANK // HD, HD]),
-                in1=table_view,
+                out=prod[:, :, first : first + width].rearrange("p e (n i h) -> p e n i h", i=PAIRS, h=2),
+                in0=acc.unsqueeze(4).to_broadcast([P, 2, width // HD, PAIRS, 2]),
+                in1=tables,
                 op=MULT,
             )
-            rot = out_pool.tile([P, BANK // 2, 2], F32, name="rot")
-            pairs = prod[:].rearrange("p h (n j) -> p n h j", j=2)
-            nc.gpsimd.tensor_tensor(out=rot[:], in0=pairs[:, :, :, 0], in1=pairs[:, :, :, 1], op=ADD)
-            nc.sync.dma_start(out=dest, in_=rot[:].rearrange("p n h -> p (n h)"))
 
-        def q_chunk(n, m, codes, scales):
-            acc = acc_psum.tile([P, CHUNK_HEADS, HD], F32, name="acc")
+        def add_and_store(prod, dest):
+            rot = out_pool.tile([P, BANK], F32, name="rot")
+            nc.gpsimd.tensor_tensor(out=rot[:], in0=prod[:, 0], in1=prod[:, 1], op=ADD)
+            nc.sync.dma_start(out=dest, in_=rot[:] if len(dest.shape) == 2 else rot[:].rearrange("p (m c) -> p m c", m=2))
+
+        def q_tables(m, width):
+            return table[:, :, m].unsqueeze(2).to_broadcast([P, 2, width // HD, PAIRS, 2])
+
+        accs = {}
+        prods = {}
+
+        def multiply_q(n, m):
+            first, width = chunk_cols[n]
+            raw, grouped, codes, scales = chunks[n]
+            acc = acc_psum.tile([P, BANK], F32, name="acc")
+            accs[n, m] = acc
             project(
-                acc[:].rearrange("p a d -> p (a d)"),
+                acc[:, :width],
                 m,
-                [codes[:, g, :] for g in range(PASSES)],
-                [scales[:, g, :] for g in range(PASSES)],
-            )
-            rotate_and_store(
-                acc[:],
-                table[:, m].unsqueeze(2).to_broadcast([P, 2, CHUNK_HEADS, HD]),
-                q_rows[:, m, BANK * n : BANK * (n + 1)],
+                [codes[:, g] for g in range(PASSES)],
+                [scales[:, g] for g in range(PASSES)],
             )
 
-        wq0_codes, wq0_scales = quantise_wq(0, nc.vector.tensor_copy)
+        def rotate_q(n, m):
+            first, width = chunk_cols[n]
+            at = 0
+            if width < BANK:
+                at = width * (m % 2)
+            if at == 0:
+                prod = prod_pool.tile([P, 2, BANK], F32, name="prod")
+                prods[n, m] = prod
+            else:
+                prods[n, m] = prods[n, m - 1]
+            rotate_part(
+                accs[n, m][:, :width].rearrange("p (n i e) -> p e n i", i=PAIRS, e=2),
+                q_tables(m, width),
+                prods[n, m],
+                at,
+                width,
+            )
+            if at + width == BANK:
+                if width == BANK:
+                    add_and_store(prods[n, m], q_rows[:, m, first : first + width])
+                else:
+                    add_and_store(prods[n, m], q_rows[:, m - 1 : m + 1, first : first + width])
+
+        def multiply_kv(w, first):
+            raw, grouped, codes, scales = kv
+            acc = acc_psum.tile([P, BANK], F32, name="acc")
+            accs["kv", w, first] = acc
+            for a in range(GROUP_TILES):
+                project(
+                    acc[:, HD * a : HD * (a + 1)],
+                    first + a,
+                    [codes[:, g, HD * w : HD * (w + 1)] for g in range(PASSES)],
+                    [scales[:, g, HD * w : HD * (w + 1)] for g in range(PASSES)],
+                )
+
+        def rotate_k(first):
+            prod = prod_pool.tile([P, 2, BANK], F32, name="prod")
+            rotate_part(
+                accs["kv", 0, first][:].rearrange("p (n i e) -> p e n i", i=PAIRS, e=2),
+                table[:, :, first : first + GROUP_TILES],
+                prod,
+                0,
+                BANK,
+            )
+            add_and_store(prod, k_rows[:, first : first + GROUP_TILES, :].rearrange("p m d -> p (m d)"))
+
+        def store_v(first):
+            v_sb = out_pool.tile([P, BANK], F32, name="v_sb")
+            nc.scalar.copy(out=v_sb[:], in_=accs["kv", 1, first][:])
+            nc.sync.dma_start(
+                out=v_rows[:, first : first + GROUP_TILES, :].rearrange("p m d -> p (m d)"), in_=v_sb[:]
+            )
+
+        vec = nc.vector.tensor_copy
+        sca = nc.scalar.copy
+
+        turn_x(0)
+        regroup(vec, chunks[0], 0, 0, 256)
+        copy_x(0)
         quantise_x(0)
-        for m in range(TILES):
+        regroup(sca, chunks[0], 1, 128, 256)
+        regroup(vec, chunks[0], 1, 0, 128)
+        quantise_weights(chunks[0], 0)
+        quantise_weights(chunks[0], 1)
+        turn_x(1)
+        copy_x(1)
+        multiply_q(0, 0)
+        turn_x(2)
+        copy_x(2)
+        rotate_q(0, 0)
+        quantise_x(1)
+        for m in range(1, TILES):
+            if m + 2 < TILES:
+                turn_x(m + 2)
+                copy_x(m + 2)
+            multiply_q(0, m)
             if m + 1 < TILES:
                 quantise_x(m + 1)
-            q_chunk(0, m, wq0_codes, wq0_scales)
-
-        kv_codes, kv_scales = quantise_kv()
-        wq1_codes, wq1_scales = quantise_wq(1, nc.scalar.copy)
-
+            rotate_q(0, m)
+        for g in range(PASSES):
+            regroup(sca, chunks[1], g, 0, 256)
+        for g in range(PASSES):
+            quantise_weights(chunks[1], g)
+        regroup(sca, kv, 0, 0, 256)
+        regroup(sca, kv, 1, 0, 256)
+        for g in range(PASSES):
+            for h in range(2):
+                regroup(sca, chunks[2], g, 256 * h, 256 * (h + 1))
+        for m in range(TILES):
+            multiply_q(1, m)
+            if m == 4:
+                quantise_weights(kv, 0)
+            if m == 6:
+                quantise_weights(kv, 1)
+            rotate_q(1, m)
         for w in range(2):
             for first in range(0, TILES, GROUP_TILES):
-                acc = acc_psum.tile([P, GROUP_TILES, HD], F32, name="acc")
-                for a in range(GROUP_TILES):
-                    project(
-                        acc[:, a, :],
-                        first + a,
-                        [kv_codes[:, w, g, :] for g in range(PASSES)],
-                        [kv_scales[:, w, g, :] for g in range(PASSES)],
-                    )
-                if w == 0:
-                    rotate_and_store(
-                        acc[:],
-                        table[:, first : first + GROUP_TILES].rearrange("p m h d -> p h m d"),
-                        k_rows[:, first : first + GROUP_TILES, :].rearrange("p m d -> p (m d)"),
-                    )
-                else:
-                    v_sb = out_pool.tile([P, GROUP_TILES, HD], F32, name="v_sb")
-                    nc.scalar.copy(out=v_sb[:], in_=acc[:])
-                    nc.sync.dma_start(out=v_rows[:, first : first + GROUP_TILES, :], in_=v_sb[:])
-
+                multiply_kv(w, first)
+        for first in range(0, TILES, GROUP_TILES):
+            store_v(first)
+        for first in range(0, TILES, GROUP_TILES):
+            quantise_weights(chunks[2], first // GROUP_TILES)
+            rotate_k(first)
         for m in range(TILES):
-            q_chunk(1, m, wq1_codes, wq1_scales)
+            multiply_q(2, m)
+            rotate_q(2, m)

@@ -164,8 +164,8 @@ def tile_attention_pa_kernel(tc, x, Wq, Wk, Wv, cos, sin, out_0, out_1, out_2):
         def rotate_part(acc, tables, prod, first, width):
             nc.vector.tensor_tensor(
                 out=prod[:, :, first : first + width].rearrange("p e (n i h) -> p e n i h", i=PAIRS, h=2),
-                in0=acc.unsqueeze(4).to_broadcast([P, 2, width // HD, PAIRS, 2]),
-                in1=tables,
+                in0=tables,
+                in1=acc.unsqueeze(4).to_broadcast([P, 2, width // HD, PAIRS, 2]),
                 op=MULT,
             )
 

@@ -41,73 +41,78 @@ def tile_attention_pa_kernel(tc, x, Wq, Wk, Wv, cos, sin, out_0, out_1, out_2):
         consts = stack.enter_context(tc.tile_pool(name="consts", bufs=1))
         x_pool = stack.enter_context(tc.tile_pool(name="x_pool", bufs=TILES))
         prod_pool = stack.enter_context(tc.tile_pool(name="prod_pool", bufs=4))
-        out_pool = stack.enter_context(tc.tile_pool(name="out_pool", bufs=8))
+        out_pool = stack.enter_context(tc.tile_pool(name="out_pool", bufs=10))
         turn_psum = stack.enter_context(tc.psum_pool(name="turn_psum", bufs=3))
         acc_psum = stack.enter_context(tc.psum_pool(name="acc_psum", bufs=5))
         stack.enter_context(tc.manual_schedule())
 
-        def weight_tiles(tag, width):
-            raw = consts.tile([P, PASSES, PACK, width], BF16, name=tag + "_raw")
+        def weight_tiles(tag, width, raw):
             grouped = consts.tile([P, PASSES, width, PACK], BF16, name=tag + "_grouped", align_bytes=64)
             codes = consts.tile([P, PASSES, width], U32, name=tag + "_codes", align_bytes=64)
             scales = consts.tile([P, PASSES, width], U8, name=tag + "_scales", align_bytes=64)
             return raw, grouped, codes, scales
 
         chunk_cols = [(0, 256), (256, 256), (512, 512)]
-        chunks = [weight_tiles("q%d" % n, width) for n, (first, width) in enumerate(chunk_cols)]
-        kv = weight_tiles("kv", 2 * HD)
-        x_raw = [x_pool.tile([P, D], BF16, name="x_raw") for m in range(TILES)]
+        first_raw = consts.tile([P, PASSES, PACK, 256], BF16)
+        rest_raw = consts.tile([P, PASSES, PACK, HEADS * HD - 256], BF16)
+        kv_raw = consts.tile([P, 2, PASSES, PACK, HD], BF16)
+        chunks = [
+            weight_tiles("q0", 256, lambda g, a, b: first_raw[:, g, :, a:b]),
+            weight_tiles("q1", 256, lambda g, a, b: rest_raw[:, g, :, a:b]),
+            weight_tiles("q2", 512, lambda g, a, b: rest_raw[:, g, :, 256 + a : 256 + b]),
+        ]
+        kv = weight_tiles("kv", 2 * HD, lambda g, a, b: kv_raw[:, a // HD, g])
+        x_raw = consts.tile([P, TILES, D], BF16)
+        rot_first = consts.tile([P, TILES, BANK], F32)
         planes = consts.tile([P, 3, TILES, PAIRS], BF16)
         table = consts.tile([P, 2, TILES, PAIRS, 2], BF16)
 
-        def load_x(m):
-            nc.sync.dma_start(out=x_raw[m][:], in_=x_rows[:, m, :])
+        def load_x(first, last):
+            nc.sync.dma_start(out=x_raw[:, first:last], in_=x_rows[:, first:last, :])
 
-        def load_q(n):
-            first, width = chunk_cols[n]
-            for g in range(PASSES):
-                nc.sync.dma_start(
-                    out=chunks[n][0][:, g],
-                    in_=Wq[K_PASS * g : K_PASS * (g + 1), first : first + width].rearrange(
-                        "(p t) c -> p t c", t=PACK
-                    ),
-                )
-
-        def load_kv():
-            for w, weight in enumerate((Wk, Wv)):
-                for g in range(PASSES):
-                    nc.sync.dma_start(
-                        out=kv[0][:, g, :, HD * w : HD * (w + 1)],
-                        in_=weight[K_PASS * g : K_PASS * (g + 1), :].rearrange("(p t) c -> p t c", t=PACK),
-                    )
+        def load_q(raw, g, first, last):
+            nc.sync.dma_start(
+                out=raw[:, g],
+                in_=Wq[K_PASS * g : K_PASS * (g + 1), first:last].rearrange("(p t) c -> p t c", t=PACK),
+            )
 
         nc.scalar.dma_start(out=planes[:, 2], in_=sin_rows)
         nc.scalar.dma_start(out=planes[:, 1], in_=cos_rows)
-        load_x(0)
-        load_q(0)
-        for m in range(1, TILES):
-            load_x(m)
-        load_q(1)
-        load_kv()
-        load_q(2)
+        load_x(0, 1)
+        for g in range(PASSES):
+            load_q(first_raw, g, 0, 256)
+        load_x(1, 2)
+        for m in range(2, TILES, 2):
+            load_x(m, m + 2)
+        for g in range(PASSES):
+            load_q(rest_raw, g, 256, HEADS * HD)
+        for w, weight in enumerate((Wk, Wv)):
+            nc.sync.dma_start(
+                out=kv_raw[:, w].rearrange("p g t c -> p g (t c)"),
+                in_=weight.rearrange("(g p t) c -> p g (t c)", p=P, t=PACK),
+            )
 
         ident = consts.tile([P, P], F32)
         make_identity(nc, ident[:])
-        for first, last in ((0, 2), (2, TILES)):
+        def interleaved(e, first, last):
+            return table[:, e, first:last], planes[:, 1 - e : 3 - e, first:last].rearrange("p h m i -> p m i h")
 
-            def scaled(out, in_, factor):
-                nc.gpsimd.tensor_scalar(out=out, in0=in_, scalar1=factor, scalar2=0.0, op0=MULT, op1=ADD)
-
-            scaled(planes[:, 0, first:last], planes[:, 2, first:last], -1.0)
+        nc.scalar.mul(out=planes[:, 0, 0:2], in_=planes[:, 2, 0:2], mul=-1.0)
+        for e in range(2):
+            out, in_ = interleaved(e, 0, 2)
+            nc.scalar.copy(out=out, in_=in_)
+        nc.gpsimd.tensor_scalar(
+            out=planes[:, 0, 2:TILES], in0=planes[:, 2, 2:TILES], scalar1=-1.0, scalar2=0.0, op0=MULT, op1=ADD
+        )
+        for m in range(2, TILES, 2):
             for e in range(2):
-                scaled(
-                    table[:, e, first:last], planes[:, 1 - e : 3 - e, first:last].rearrange("p h m i -> p m i h"), 1.0
-                )
+                out, in_ = interleaved(e, m, m + 2)
+                nc.gpsimd.tensor_scalar(out=out, in0=in_, scalar1=1.0, scalar2=0.0, op0=MULT, op1=ADD)
 
         def regroup(copy_engine, tiles, g, first, last):
             raw, grouped = tiles[:2]
             copy_engine(
-                out=grouped[:, g, first:last, :], in_=raw[:, g, :, first:last].rearrange("p t c -> p c t")
+                out=grouped[:, g, first:last, :], in_=raw(g, first, last).rearrange("p t c -> p c t")
             )
 
         def quantise_weights(tiles, g):
@@ -125,7 +130,7 @@ def tile_attention_pa_kernel(tc, x, Wq, Wk, Wv, cos, sin, out_0, out_1, out_2):
         turned_x = {}
 
         def turn_x(m):
-            words = x_raw[m][:].bitcast(F32)
+            words = x_raw[:, m].bitcast(F32)
             turned = turn_psum.tile([P, PASSES, 2, P], F32, name="turned")
             for g in range(PASSES):
                 for u in range(2):
@@ -169,10 +174,10 @@ def tile_attention_pa_kernel(tc, x, Wq, Wk, Wv, cos, sin, out_0, out_1, out_2):
                 op=MULT,
             )
 
-        def add_and_store(prod, dest):
+        def add_and_store(engine, prod, dest):
             rot = out_pool.tile([P, BANK], F32, name="rot")
-            nc.gpsimd.tensor_tensor(out=rot[:], in0=prod[:, 0], in1=prod[:, 1], op=ADD)
-            nc.sync.dma_start(out=dest, in_=rot[:] if len(dest.shape) == 2 else rot[:].rearrange("p (m c) -> p m c", m=2))
+            engine.tensor_tensor(out=rot[:], in0=prod[:, 0], in1=prod[:, 1], op=ADD)
+            nc.sync.dma_start(out=dest, in_=rot[:])
 
         def q_tables(m, width):
             return table[:, :, m].unsqueeze(2).to_broadcast([P, 2, width // HD, PAIRS, 2])
@@ -209,11 +214,19 @@ def tile_attention_pa_kernel(tc, x, Wq, Wk, Wv, cos, sin, out_0, out_1, out_2):
                 at,
                 width,
             )
-            if at + width == BANK:
-                if width == BANK:
-                    add_and_store(prods[n, m], q_rows[:, m, first : first + width])
-                else:
-                    add_and_store(prods[n, m], q_rows[:, m - 1 : m + 1, first : first + width])
+            if width < BANK and at > 0:
+                nc.gpsimd.tensor_tensor(
+                    out=rot_first[:, m - 1 : m + 1, first : first + width],
+                    in0=prods[n, m][:, 0].rearrange("p (m c) -> p m c", m=2),
+                    in1=prods[n, m][:, 1].rearrange("p (m c) -> p m c", m=2),
+                    op=ADD,
+                )
+                if n == 1:
+                    nc.sync.dma_start(out=q_rows[:, m - 1 : m + 1, 0:BANK], in_=rot_first[:, m - 1 : m + 1])
+
+        def finish_q(engine, n, m):
+            first, width = chunk_cols[n]
+            add_and_store(engine, prods[n, m], q_rows[:, m, first : first + width])
 
         def multiply_kv(w, first):
             raw, grouped, codes, scales = kv
@@ -236,7 +249,7 @@ def tile_attention_pa_kernel(tc, x, Wq, Wk, Wv, cos, sin, out_0, out_1, out_2):
                 0,
                 BANK,
             )
-            add_and_store(prod, k_rows[:, first : first + GROUP_TILES, :].rearrange("p m d -> p (m d)"))
+            add_and_store(nc.gpsimd, prod, k_rows[:, first : first + GROUP_TILES, :].rearrange("p m d -> p (m d)"))
 
         def store_v(first):
             v_sb = out_pool.tile([P, BANK], F32, name="v_sb")
@@ -275,8 +288,9 @@ def tile_attention_pa_kernel(tc, x, Wq, Wk, Wv, cos, sin, out_0, out_1, out_2):
             regroup(sca, chunks[1], g, 0, 256)
         for g in range(PASSES):
             quantise_weights(chunks[1], g)
-        regroup(sca, kv, 0, 0, 256)
-        regroup(sca, kv, 1, 0, 256)
+        for g in range(PASSES):
+            for w in range(2):
+                regroup(sca, kv, g, HD * w, HD * (w + 1))
         for g in range(PASSES):
             for h in range(2):
                 regroup(sca, chunks[2], g, 256 * h, 256 * (h + 1))
@@ -298,3 +312,7 @@ def tile_attention_pa_kernel(tc, x, Wq, Wk, Wv, cos, sin, out_0, out_1, out_2):
         for m in range(TILES):
             multiply_q(2, m)
             rotate_q(2, m)
+            if m < TILES - 2:
+                finish_q(nc.gpsimd, 2, m)
+        for m in range(TILES - 2, TILES):
+            finish_q(nc.vector, 2, m)

@@ -65,7 +65,7 @@ def tile_attention_pa_kernel(tc, x, Wq, Wk, Wv, cos, sin, out_0, out_1, out_2):
         x_raw = consts.tile([P, TILES, D], BF16)
         rot_first = consts.tile([P, TILES, BANK], F32)
         planes = consts.tile([P, 3, TILES, PAIRS], BF16)
-        table = consts.tile([P, 2, TILES, PAIRS, 2], BF16)
+        table = consts.tile([P, TILES, 2, PAIRS, 2], F32)
 
         def load_x(first, last):
             nc.sync.dma_start(out=x_raw[:, first:last], in_=x_rows[:, first:last, :])
@@ -76,8 +76,8 @@ def tile_attention_pa_kernel(tc, x, Wq, Wk, Wv, cos, sin, out_0, out_1, out_2):
                 in_=Wq[K_PASS * g : K_PASS * (g + 1), first:last].rearrange("(p t) c -> p t c", t=PACK),
             )
 
-        nc.scalar.dma_start(out=planes[:, 2], in_=sin_rows)
-        nc.scalar.dma_start(out=planes[:, 1], in_=cos_rows)
+        nc.scalar.dma_start(out=planes[:, 1], in_=sin_rows)
+        nc.scalar.dma_start(out=planes[:, 0], in_=cos_rows)
         load_x(0, 1)
         for g in range(PASSES):
             load_q(first_raw, g, 0, 256)
@@ -95,14 +95,18 @@ def tile_attention_pa_kernel(tc, x, Wq, Wk, Wv, cos, sin, out_0, out_1, out_2):
         ident = consts.tile([P, P], F32)
         make_identity(nc, ident[:])
         def interleaved(e, first, last):
-            return table[:, e, first:last], planes[:, 1 - e : 3 - e, first:last].rearrange("p h m i -> p m i h")
+            if e == 0:
+                source = planes[:, 0, first:last].unsqueeze(3).to_broadcast([P, last - first, PAIRS, 2])
+            else:
+                source = planes[:, 1:3, first:last].rearrange("p h m i -> p m i h")
+            return table[:, first:last, e], source
 
-        nc.scalar.mul(out=planes[:, 0, 0:2], in_=planes[:, 2, 0:2], mul=-1.0)
+        nc.scalar.mul(out=planes[:, 2, 0:2], in_=planes[:, 1, 0:2], mul=-1.0)
         for e in range(2):
             out, in_ = interleaved(e, 0, 2)
             nc.scalar.copy(out=out, in_=in_)
         nc.gpsimd.tensor_scalar(
-            out=planes[:, 0, 2:TILES], in0=planes[:, 2, 2:TILES], scalar1=-1.0, scalar2=0.0, op0=MULT, op1=ADD
+            out=planes[:, 2, 2:TILES], in0=planes[:, 1, 2:TILES], scalar1=-1.0, scalar2=0.0, op0=MULT, op1=ADD
         )
         for m in range(2, TILES, 2):
             for e in range(2):
@@ -168,19 +172,29 @@ def tile_attention_pa_kernel(tc, x, Wq, Wk, Wv, cos, sin, out_0, out_1, out_2):
 
         def rotate_part(acc, tables, prod, first, width):
             nc.vector.tensor_tensor(
-                out=prod[:, :, first : first + width].rearrange("p e (n i h) -> p e n i h", i=PAIRS, h=2),
-                in0=tables,
-                in1=acc.unsqueeze(4).to_broadcast([P, 2, width // HD, PAIRS, 2]),
+                out=prod[:, :, first : first + width].rearrange("p h (n d) -> p h n d", d=HD),
+                in0=acc.unsqueeze(1).to_broadcast([P, 2, width // HD, HD]),
+                in1=tables,
                 op=MULT,
+            )
+
+        def add_pairs(engine, out, prod):
+            engine.tensor_tensor(
+                out=out.rearrange("p (n h) -> p n h", h=2),
+                in0=prod[:, 0].rearrange("p (n h) -> p n h", h=2),
+                in1=prod[:, 1].rearrange("p (n h) -> p n h", h=2)[:, :, ::-1],
+                op=ADD,
             )
 
         def add_and_store(engine, prod, dest):
             rot = out_pool.tile([P, BANK], F32, name="rot")
-            engine.tensor_tensor(out=rot[:], in0=prod[:, 0], in1=prod[:, 1], op=ADD)
+            add_pairs(engine, rot[:], prod)
             nc.sync.dma_start(out=dest, in_=rot[:])
 
         def q_tables(m, width):
-            return table[:, :, m].unsqueeze(2).to_broadcast([P, 2, width // HD, PAIRS, 2])
+            return (
+                table[:, m].rearrange("p h i j -> p h (i j)").unsqueeze(2).to_broadcast([P, 2, width // HD, HD])
+            )
 
         accs = {}
         prods = {}
@@ -208,7 +222,7 @@ def tile_attention_pa_kernel(tc, x, Wq, Wk, Wv, cos, sin, out_0, out_1, out_2):
             else:
                 prods[n, m] = prods[n, m - 1]
             rotate_part(
-                accs[n, m][:, :width].rearrange("p (n i e) -> p e n i", i=PAIRS, e=2),
+                accs[n, m][:, :width].rearrange("p (n d) -> p n d", d=HD),
                 q_tables(m, width),
                 prods[n, m],
                 at,
@@ -216,9 +230,9 @@ def tile_attention_pa_kernel(tc, x, Wq, Wk, Wv, cos, sin, out_0, out_1, out_2):
             )
             if width < BANK and at > 0:
                 nc.gpsimd.tensor_tensor(
-                    out=rot_first[:, m - 1 : m + 1, first : first + width],
-                    in0=prods[n, m][:, 0].rearrange("p (m c) -> p m c", m=2),
-                    in1=prods[n, m][:, 1].rearrange("p (m c) -> p m c", m=2),
+                    out=rot_first[:, m - 1 : m + 1, first : first + width].rearrange("p m (n h) -> p m n h", h=2),
+                    in0=prods[n, m][:, 0].rearrange("p (m n h) -> p m n h", m=2, h=2),
+                    in1=prods[n, m][:, 1].rearrange("p (m n h) -> p m n h", m=2, h=2)[:, :, :, ::-1],
                     op=ADD,
                 )
                 if n == 1:
@@ -243,8 +257,8 @@ def tile_attention_pa_kernel(tc, x, Wq, Wk, Wv, cos, sin, out_0, out_1, out_2):
         def rotate_k(first):
             prod = prod_pool.tile([P, 2, BANK], F32, name="prod")
             rotate_part(
-                accs["kv", 0, first][:].rearrange("p (n i e) -> p e n i", i=PAIRS, e=2),
-                table[:, :, first : first + GROUP_TILES],
+                accs["kv", 0, first][:].rearrange("p (n d) -> p n d", d=HD),
+                table[:, first : first + GROUP_TILES].rearrange("p m h i j -> p h m (i j)"),
                 prod,
                 0,
                 BANK,

@@ -40,10 +40,11 @@ def tile_attention_pa_kernel(tc, x, Wq, Wk, Wv, cos, sin, out_0, out_1, out_2):
     with ExitStack() as stack:
         consts = stack.enter_context(tc.tile_pool(name="consts", bufs=1))
         x_pool = stack.enter_context(tc.tile_pool(name="x_pool", bufs=TILES))
-        prod_pool = stack.enter_context(tc.tile_pool(name="prod_pool", bufs=4))
+        prod_pool = stack.enter_context(tc.tile_pool(name="prod_pool", bufs=10))
         out_pool = stack.enter_context(tc.tile_pool(name="out_pool", bufs=10))
         turn_psum = stack.enter_context(tc.psum_pool(name="turn_psum", bufs=3))
-        acc_psum = stack.enter_context(tc.psum_pool(name="acc_psum", bufs=5))
+        acc_psum = stack.enter_context(tc.psum_pool(name="acc_psum", bufs=4))
+        idle_psum = stack.enter_context(tc.psum_pool(name="idle_psum", bufs=1))
         stack.enter_context(tc.manual_schedule())
 
         def weight_tiles(tag, width, raw):
@@ -76,12 +77,16 @@ def tile_attention_pa_kernel(tc, x, Wq, Wk, Wv, cos, sin, out_0, out_1, out_2):
                 in_=Wq[K_PASS * g : K_PASS * (g + 1), first:last].rearrange("(p t) c -> p t c", t=PACK),
             )
 
-        nc.scalar.dma_start(out=planes[:, 1], in_=sin_rows)
-        nc.scalar.dma_start(out=planes[:, 0], in_=cos_rows)
+        def load_tables(queue, first, last):
+            queue.dma_start(out=planes[:, 1, first:last], in_=sin_rows[:, first:last])
+            queue.dma_start(out=planes[:, 0, first:last], in_=cos_rows[:, first:last])
+
+        load_tables(nc.scalar, 0, 2)
         load_x(0, 1)
         for g in range(PASSES):
             load_q(first_raw, g, 0, 256)
         load_x(1, 2)
+        load_tables(nc.sync, 2, TILES)
         for m in range(2, TILES, 2):
             load_x(m, m + 2)
         for g in range(PASSES):
@@ -105,10 +110,15 @@ def tile_attention_pa_kernel(tc, x, Wq, Wk, Wv, cos, sin, out_0, out_1, out_2):
         for e in range(2):
             out, in_ = interleaved(e, 0, 2)
             nc.scalar.copy(out=out, in_=in_)
-        nc.gpsimd.tensor_scalar(
-            out=planes[:, 2, 2:TILES], in0=planes[:, 1, 2:TILES], scalar1=-1.0, scalar2=0.0, op0=MULT, op1=ADD
-        )
         for m in range(2, TILES, 2):
+            nc.gpsimd.tensor_scalar(
+                out=planes[:, 2, m : m + 2],
+                in0=planes[:, 1, m : m + 2],
+                scalar1=-1.0,
+                scalar2=0.0,
+                op0=MULT,
+                op1=ADD,
+            )
             for e in range(2):
                 out, in_ = interleaved(e, m, m + 2)
                 nc.gpsimd.tensor_scalar(out=out, in0=in_, scalar1=1.0, scalar2=0.0, op0=MULT, op1=ADD)
@@ -119,12 +129,12 @@ def tile_attention_pa_kernel(tc, x, Wq, Wk, Wv, cos, sin, out_0, out_1, out_2):
                 out=grouped[:, g, first:last, :], in_=raw(g, first, last).rearrange("p t c -> p c t")
             )
 
-        def quantise_weights(tiles, g):
+        def quantise_weights(tiles, first, last):
             raw, grouped, codes, scales = tiles
             nc.vector.quantize_mx(
-                out=codes[:, g].bitcast(FP8X4),
-                scales=scales[:, g],
-                in_=grouped[:, g].rearrange("p c t -> p (c t)"),
+                out=codes[:, first:last].rearrange("p g c -> p (g c)").bitcast(FP8X4),
+                scales=scales[:, first:last].rearrange("p g c -> p (g c)"),
+                in_=grouped[:, first:last].rearrange("p g c t -> p (g c t)"),
             )
 
         x_grouped = {}
@@ -228,15 +238,17 @@ def tile_attention_pa_kernel(tc, x, Wq, Wk, Wv, cos, sin, out_0, out_1, out_2):
                 at,
                 width,
             )
-            if width < BANK and at > 0:
-                nc.gpsimd.tensor_tensor(
-                    out=rot_first[:, m - 1 : m + 1, first : first + width].rearrange("p m (n h) -> p m n h", h=2),
-                    in0=prods[n, m][:, 0].rearrange("p (m n h) -> p m n h", m=2, h=2),
-                    in1=prods[n, m][:, 1].rearrange("p (m n h) -> p m n h", m=2, h=2)[:, :, :, ::-1],
-                    op=ADD,
-                )
-                if n == 1:
-                    nc.sync.dma_start(out=q_rows[:, m - 1 : m + 1, 0:BANK], in_=rot_first[:, m - 1 : m + 1])
+
+        def finish_first(n, m, engine):
+            first, width = chunk_cols[n]
+            engine.tensor_tensor(
+                out=rot_first[:, m : m + 2, first : first + width].rearrange("p m (n h) -> p m n h", h=2),
+                in0=prods[n, m][:, 0].rearrange("p (m n h) -> p m n h", m=2, h=2),
+                in1=prods[n, m][:, 1].rearrange("p (m n h) -> p m n h", m=2, h=2)[:, :, :, ::-1],
+                op=ADD,
+            )
+            if n == 1:
+                nc.sync.dma_start(out=q_rows[:, m : m + 2, 0:BANK], in_=rot_first[:, m : m + 2])
 
         def finish_q(engine, n, m):
             first, width = chunk_cols[n]
@@ -263,7 +275,12 @@ def tile_attention_pa_kernel(tc, x, Wq, Wk, Wv, cos, sin, out_0, out_1, out_2):
                 0,
                 BANK,
             )
-            add_and_store(nc.gpsimd, prod, k_rows[:, first : first + GROUP_TILES, :].rearrange("p m d -> p (m d)"))
+            prods["k", first] = prod
+
+        def finish_k(engine, first):
+            add_and_store(
+                engine, prods["k", first], k_rows[:, first : first + GROUP_TILES, :].rearrange("p m d -> p (m d)")
+            )
 
         def store_v(first):
             v_sb = out_pool.tile([P, BANK], F32, name="v_sb")
@@ -272,18 +289,26 @@ def tile_attention_pa_kernel(tc, x, Wq, Wk, Wv, cos, sin, out_0, out_1, out_2):
                 out=v_rows[:, first : first + GROUP_TILES, :].rearrange("p m d -> p (m d)"), in_=v_sb[:]
             )
 
+        idle = idle_psum.tile([P, P], F32)
+
+        def keep_warm(count):
+            for n in range(count):
+                nc.tensor.matmul(idle[:], ident[:], ident[:], start=True, stop=True)
+
         vec = nc.vector.tensor_copy
         sca = nc.scalar.copy
 
         turn_x(0)
+        keep_warm(3)
         regroup(vec, chunks[0], 0, 0, 256)
         copy_x(0)
         quantise_x(0)
         regroup(sca, chunks[0], 1, 128, 256)
         regroup(vec, chunks[0], 1, 0, 128)
-        quantise_weights(chunks[0], 0)
-        quantise_weights(chunks[0], 1)
+        quantise_weights(chunks[0], 0, 1)
+        quantise_weights(chunks[0], 1, 2)
         turn_x(1)
+        keep_warm(1)
         copy_x(1)
         multiply_q(0, 0)
         turn_x(2)
@@ -293,40 +318,45 @@ def tile_attention_pa_kernel(tc, x, Wq, Wk, Wv, cos, sin, out_0, out_1, out_2):
         for m in range(1, TILES):
             if m + 2 < TILES:
                 turn_x(m + 2)
+                keep_warm(1)
                 copy_x(m + 2)
             multiply_q(0, m)
             if m + 1 < TILES:
                 quantise_x(m + 1)
             rotate_q(0, m)
+            if m in (2, 4, 6):
+                finish_first(0, m - 2, nc.vector)
+        finish_first(0, 6, nc.gpsimd)
         for g in range(PASSES):
             regroup(sca, chunks[1], g, 0, 256)
-        for g in range(PASSES):
-            quantise_weights(chunks[1], g)
         for g in range(PASSES):
             for w in range(2):
                 regroup(sca, kv, g, HD * w, HD * (w + 1))
         for g in range(PASSES):
             for h in range(2):
                 regroup(sca, chunks[2], g, 256 * h, 256 * (h + 1))
+        quantise_weights(chunks[1], 0, 2)
         for m in range(TILES):
             multiply_q(1, m)
             if m == 4:
-                quantise_weights(kv, 0)
-            if m == 6:
-                quantise_weights(kv, 1)
+                quantise_weights(kv, 0, 2)
             rotate_q(1, m)
+            if m % 2 == 1:
+                finish_first(1, m - 1, nc.gpsimd)
         for w in range(2):
             for first in range(0, TILES, GROUP_TILES):
                 multiply_kv(w, first)
         for first in range(0, TILES, GROUP_TILES):
             store_v(first)
+        rotate_k(0)
+        quantise_weights(chunks[2], 0, 2)
+        rotate_k(GROUP_TILES)
         for first in range(0, TILES, GROUP_TILES):
-            quantise_weights(chunks[2], first // GROUP_TILES)
-            rotate_k(first)
+            finish_k(nc.gpsimd, first)
         for m in range(TILES):
             multiply_q(2, m)
             rotate_q(2, m)
-            if m < TILES - 2:
+            if m < 6:
                 finish_q(nc.gpsimd, 2, m)
-        for m in range(TILES - 2, TILES):
+        for m in range(6, TILES):
             finish_q(nc.vector, 2, m)

@@ -55,12 +55,13 @@ def tile_attention_pa_kernel(tc, x, Wq, Wk, Wv, cos, sin, out_0, out_1, out_2):
 
         chunk_cols = [(0, 256), (256, 256), (512, 512)]
         first_raw = consts.tile([P, PASSES, PACK, 256], BF16)
-        rest_raw = consts.tile([P, PASSES, PACK, HEADS * HD - 256], BF16)
+        second_raw = consts.tile([P, PASSES, PACK, 256], BF16)
+        last_raw = consts.tile([P, PASSES, PACK, BANK], BF16)
         kv_raw = consts.tile([P, 2, PASSES, PACK, HD], BF16)
         chunks = [
             weight_tiles("q0", 256, lambda g, a, b: first_raw[:, g, :, a:b]),
-            weight_tiles("q1", 256, lambda g, a, b: rest_raw[:, g, :, a:b]),
-            weight_tiles("q2", 512, lambda g, a, b: rest_raw[:, g, :, 256 + a : 256 + b]),
+            weight_tiles("q1", 256, lambda g, a, b: second_raw[:, g, :, a:b]),
+            weight_tiles("q2", 512, lambda g, a, b: last_raw[:, g, :, a:b]),
         ]
         kv = weight_tiles("kv", 2 * HD, lambda g, a, b: kv_raw[:, a // HD, g])
         x_raw = consts.tile([P, TILES, D], BF16)
@@ -87,15 +88,18 @@ def tile_attention_pa_kernel(tc, x, Wq, Wk, Wv, cos, sin, out_0, out_1, out_2):
             load_q(first_raw, g, 0, 256)
         load_x(1, 2)
         load_tables(nc.sync, 2, TILES)
-        for m in range(2, TILES, 2):
-            load_x(m, m + 2)
+        load_x(2, 4)
+        load_x(4, 6)
         for g in range(PASSES):
-            load_q(rest_raw, g, 256, HEADS * HD)
+            load_q(second_raw, g, 256, 512)
+        load_x(6, 8)
         for w, weight in enumerate((Wk, Wv)):
             nc.sync.dma_start(
                 out=kv_raw[:, w].rearrange("p g t c -> p g (t c)"),
                 in_=weight.rearrange("(g p t) c -> p g (t c)", p=P, t=PACK),
             )
+        for g in range(PASSES):
+            load_q(last_raw, g, 512, HEADS * HD)
 
         ident = consts.tile([P, P], F32)
         make_identity(nc, ident[:])
@@ -318,24 +322,26 @@ def tile_attention_pa_kernel(tc, x, Wq, Wk, Wv, cos, sin, out_0, out_1, out_2):
         for m in range(1, TILES):
             if m + 2 < TILES:
                 turn_x(m + 2)
-                keep_warm(1)
+                keep_warm(m % 2)
                 copy_x(m + 2)
+                if m + 2 in (3, 4, 5, 6):
+                    at = (3, 4, 5, 6).index(m + 2)
+                    regroup(sca, chunks[1], at // 2, 128 * (at % 2), 128 * (at % 2) + 128)
             multiply_q(0, m)
             if m + 1 < TILES:
                 quantise_x(m + 1)
+            if m == TILES - 1:
+                quantise_weights(chunks[1], 0, 2)
             rotate_q(0, m)
             if m in (2, 4, 6):
                 finish_first(0, m - 2, nc.vector)
         finish_first(0, 6, nc.gpsimd)
-        for g in range(PASSES):
-            regroup(sca, chunks[1], g, 0, 256)
         for g in range(PASSES):
             for w in range(2):
                 regroup(sca, kv, g, HD * w, HD * (w + 1))
         for g in range(PASSES):
             for h in range(2):
                 regroup(sca, chunks[2], g, 256 * h, 256 * (h + 1))
-        quantise_weights(chunks[1], 0, 2)
         for m in range(TILES):
             multiply_q(1, m)
             if m == 4:

from contextlib import ExitStack

from concourse import mybir
from concourse.masks import make_identity

F32 = mybir.dt.float32
BF16 = mybir.dt.bfloat16
U32 = mybir.dt.uint32
U8 = mybir.dt.uint8
FP8X4 = mybir.dt.float8_e4m3fn_x4
MULT = mybir.AluOpType.mult
ADD = mybir.AluOpType.add

P = 128
T = 1024
D = 1024
HEADS = 8
HD = 128
PAIRS = HD // 2
PACK = 4
K_PASS = P * PACK
PASSES = D // K_PASS
TILES = T // P
BANK = 512
GROUP_TILES = BANK // HD

FLOPS = 2 * T * D * (HEADS * HD + 2 * HD)


def tile_attention_pa_kernel(tc, x, Wq, Wk, Wv, cos, sin, out_0, out_1, out_2):
    nc = tc.nc

    x_rows = x.flatten_outer_dims().rearrange("(p m) k -> p m k", m=TILES)
    cos_rows = cos.rearrange("(p m) i -> p m i", m=TILES)
    sin_rows = sin.rearrange("(p m) i -> p m i", m=TILES)
    q_rows = out_0.rearrange("b t h d -> (b t) (h d)").rearrange("(p m) c -> p m c", m=TILES)
    k_rows = out_1.flatten_outer_dims().rearrange("(p m) d -> p m d", m=TILES)
    v_rows = out_2.flatten_outer_dims().rearrange("(p m) d -> p m d", m=TILES)

    with ExitStack() as stack:
        consts = stack.enter_context(tc.tile_pool(name="consts", bufs=1))
        x_pool = stack.enter_context(tc.tile_pool(name="x_pool", bufs=TILES))
        prod_pool = stack.enter_context(tc.tile_pool(name="prod_pool", bufs=10))
        out_pool = stack.enter_context(tc.tile_pool(name="out_pool", bufs=10))
        turn_psum = stack.enter_context(tc.psum_pool(name="turn_psum", bufs=3))
        acc_psum = stack.enter_context(tc.psum_pool(name="acc_psum", bufs=4))
        idle_psum = stack.enter_context(tc.psum_pool(name="idle_psum", bufs=1))
        stack.enter_context(tc.manual_schedule())

        def weight_tiles(tag, width, raw):
            grouped = consts.tile([P, PASSES, width, PACK], BF16, name=tag + "_grouped", align_bytes=64)
            codes = consts.tile([P, PASSES, width], U32, name=tag + "_codes", align_bytes=64)
            scales = consts.tile([P, PASSES, width], U8, name=tag + "_scales", align_bytes=64)
            return raw, grouped, codes, scales

        chunk_cols = [(0, 256), (256, 256), (512, 512)]
        first_raw = consts.tile([P, PASSES, PACK, 256], BF16)
        second_raw = consts.tile([P, PASSES, PACK, 256], BF16)
        last_raw = consts.tile([P, PASSES, PACK, BANK], BF16)
        kv_raw = consts.tile([P, 2, PASSES, PACK, HD], BF16)
        chunks = [
            weight_tiles("q0", 256, lambda g, a, b: first_raw[:, g, :, a:b]),
            weight_tiles("q1", 256, lambda g, a, b: second_raw[:, g, :, a:b]),
            weight_tiles("q2", 512, lambda g, a, b: last_raw[:, g, :, a:b]),
        ]
        kv = weight_tiles("kv", 2 * HD, lambda g, a, b: kv_raw[:, a // HD, g])
        x_raw = consts.tile([P, TILES, D], BF16)
        rot_first = consts.tile([P, TILES, BANK], F32)
        planes = consts.tile([P, 3, TILES, PAIRS], BF16)
        table = consts.tile([P, TILES, 2, PAIRS, 2], F32)

        def load_x(first, last):
            nc.sync.dma_start(out=x_raw[:, first:last], in_=x_rows[:, first:last, :])

        def load_q(raw, g, first, last):
            nc.sync.dma_start(
                out=raw[:, g],
                in_=Wq[K_PASS * g : K_PASS * (g + 1), first:last].rearrange("(p t) c -> p t c", t=PACK),
            )

        def load_tables(queue, first, last):
            queue.dma_start(out=planes[:, 1, first:last], in_=sin_rows[:, first:last])
            queue.dma_start(out=planes[:, 0, first:last], in_=cos_rows[:, first:last])

        load_tables(nc.scalar, 0, 2)
        load_x(0, 1)
        for g in range(PASSES):
            load_q(first_raw, g, 0, 256)
        load_x(1, 2)
        load_tables(nc.sync, 2, TILES)
        load_x(2, 4)
        load_x(4, 6)
        for g in range(PASSES):
            load_q(second_raw, g, 256, 512)
        load_x(6, 8)
        for w, weight in enumerate((Wk, Wv)):
            nc.sync.dma_start(
                out=kv_raw[:, w].rearrange("p g t c -> p g (t c)"),
                in_=weight.rearrange("(g p t) c -> p g (t c)", p=P, t=PACK),
            )
        for g in range(PASSES):
            load_q(last_raw, g, 512, HEADS * HD)

        ident = consts.tile([P, P], F32)
        make_identity(nc, ident[:])
        def interleaved(e, first, last):
            if e == 0:
                source = planes[:, 0, first:last].unsqueeze(3).to_broadcast([P, last - first, PAIRS, 2])
            else:
                source = planes[:, 1:3, first:last].rearrange("p h m i -> p m i h")
            return table[:, first:last, e], source

        nc.scalar.mul(out=planes[:, 2, 0:2], in_=planes[:, 1, 0:2], mul=-1.0)
        for e in range(2):
            out, in_ = interleaved(e, 0, 2)
            nc.scalar.copy(out=out, in_=in_)
        for m in range(2, TILES, 2):
            nc.gpsimd.tensor_scalar(
                out=planes[:, 2, m : m + 2],
                in0=planes[:, 1, m : m + 2],
                scalar1=-1.0,
                scalar2=0.0,
                op0=MULT,
                op1=ADD,
            )
            for e in range(2):
                out, in_ = interleaved(e, m, m + 2)
                nc.gpsimd.tensor_scalar(out=out, in0=in_, scalar1=1.0, scalar2=0.0, op0=MULT, op1=ADD)

        def regroup(copy_engine, tiles, g, first, last):
            raw, grouped = tiles[:2]
            copy_engine(
                out=grouped[:, g, first:last, :], in_=raw(g, first, last).rearrange("p t c -> p c t")
            )

        def quantise_weights(tiles, first, last):
            raw, grouped, codes, scales = tiles
            nc.vector.quantize_mx(
                out=codes[:, first:last].rearrange("p g c -> p (g c)").bitcast(FP8X4),
                scales=scales[:, first:last].rearrange("p g c -> p (g c)"),
                in_=grouped[:, first:last].rearrange("p g c t -> p (g c t)"),
            )

        x_grouped = {}
        x_codes = {}
        x_scales = {}

        turned_x = {}

        def turn_x(m):
            words = x_raw[:, m].bitcast(F32)
            turned = turn_psum.tile([P, PASSES, 2, P], F32, name="turned")
            for g in range(PASSES):
                for u in range(2):
                    first = 2 * P * g
                    nc.tensor.transpose(turned[:, g, u, :], words[:, first + u : first + 2 * P : 2], ident[:])
            turned_x[m] = turned

        def copy_x(m):
            x_grouped[m] = x_pool.tile([P, PASSES * P * PACK], BF16, name="x_grouped", align_bytes=64)
            nc.scalar.copy(
                out=x_grouped[m][:].bitcast(F32).rearrange("p (g r u) -> p g r u", g=PASSES, u=2),
                in_=turned_x[m][:].rearrange("p g u r -> p g r u"),
            )

        def quantise_x(m):
            x_codes[m] = x_pool.tile([P, PASSES, P], U32, name="x_codes", align_bytes=64)
            x_scales[m] = x_pool.tile([P, PASSES, P], U8, name="x_scales", align_bytes=64)
            nc.vector.quantize_mx(
                out=x_codes[m][:].rearrange("p g r -> p (g r)").bitcast(FP8X4),
                scales=x_scales[m][:].rearrange("p g r -> p (g r)"),
                in_=x_grouped[m][:],
            )

        def project(acc, m, codes, scales):
            for g in range(PASSES):
                nc.tensor.matmul_mx(
                    out=acc,
                    lhsT=x_codes[m][:, g, :].bitcast(FP8X4),
                    lhsT_scale=x_scales[m][:, g, :],
                    rhs=codes[g].bitcast(FP8X4),
                    rhs_scale=scales[g],
                    start=(g == 0),
                    stop=(g == PASSES - 1),
                )

        def rotate_part(acc, tables, prod, first, width):
            nc.vector.tensor_tensor(
                out=prod[:, :, first : first + width].rearrange("p h (n d) -> p h n d", d=HD),
                in0=acc.unsqueeze(1).to_broadcast([P, 2, width // HD, HD]),
                in1=tables,
                op=MULT,
            )

        def add_pairs(engine, out, prod):
            engine.tensor_tensor(
                out=out.rearrange("p (n h) -> p n h", h=2),
                in0=prod[:, 0].rearrange("p (n h) -> p n h", h=2),
                in1=prod[:, 1].rearrange("p (n h) -> p n h", h=2)[:, :, ::-1],
                op=ADD,
            )

        def add_and_store(engine, prod, dest):
            rot = out_pool.tile([P, BANK], F32, name="rot")
            add_pairs(engine, rot[:], prod)
            nc.sync.dma_start(out=dest, in_=rot[:])

        def q_tables(m, width):
            return (
                table[:, m].rearrange("p h i j -> p h (i j)").unsqueeze(2).to_broadcast([P, 2, width // HD, HD])
            )

        accs = {}
        prods = {}

        def multiply_q(n, m):
            first, width = chunk_cols[n]
            raw, grouped, codes, scales = chunks[n]
            acc = acc_psum.tile([P, BANK], F32, name="acc")
            accs[n, m] = acc
            project(
                acc[:, :width],
                m,
                [codes[:, g] for g in range(PASSES)],
                [scales[:, g] for g in range(PASSES)],
            )

        def rotate_q(n, m):
            first, width = chunk_cols[n]
            at = 0
            if width < BANK:
                at = width * (m % 2)
            if at == 0:
                prod = prod_pool.tile([P, 2, BANK], F32, name="prod")
                prods[n, m] = prod
            else:
                prods[n, m] = prods[n, m - 1]
            rotate_part(
                accs[n, m][:, :width].rearrange("p (n d) -> p n d", d=HD),
                q_tables(m, width),
                prods[n, m],
                at,
                width,
            )

        def finish_first(n, m, engine):
            first, width = chunk_cols[n]
            engine.tensor_tensor(
                out=rot_first[:, m : m + 2, first : first + width].rearrange("p m (n h) -> p m n h", h=2),
                in0=prods[n, m][:, 0].rearrange("p (m n h) -> p m n h", m=2, h=2),
                in1=prods[n, m][:, 1].rearrange("p (m n h) -> p m n h", m=2, h=2)[:, :, :, ::-1],
                op=ADD,
            )
            if n == 1:
                nc.sync.dma_start(out=q_rows[:, m : m + 2, 0:BANK], in_=rot_first[:, m : m + 2])

        def finish_q(engine, n, m):
            first, width = chunk_cols[n]
            add_and_store(engine, prods[n, m], q_rows[:, m, first : first + width])

        def multiply_kv(w, first):
            raw, grouped, codes, scales = kv
            acc = acc_psum.tile([P, BANK], F32, name="acc")
            accs["kv", w, first] = acc
            for a in range(GROUP_TILES):
                project(
                    acc[:, HD * a : HD * (a + 1)],
                    first + a,
                    [codes[:, g, HD * w : HD * (w + 1)] for g in range(PASSES)],
                    [scales[:, g, HD * w : HD * (w + 1)] for g in range(PASSES)],
                )

        def rotate_k(first):
            prod = prod_pool.tile([P, 2, BANK], F32, name="prod")
            rotate_part(
                accs["kv", 0, first][:].rearrange("p (n d) -> p n d", d=HD),
                table[:, first : first + GROUP_TILES].rearrange("p m h i j -> p h m (i j)"),
                prod,
                0,
                BANK,
            )
            prods["k", first] = prod

        def finish_k(engine, first):
            add_and_store(
                engine, prods["k", first], k_rows[:, first : first + GROUP_TILES, :].rearrange("p m d -> p (m d)")
            )

        def store_v(first):
            v_sb = out_pool.tile([P, BANK], F32, name="v_sb")
            nc.scalar.copy(out=v_sb[:], in_=accs["kv", 1, first][:])
            nc.sync.dma_start(
                out=v_rows[:, first : first + GROUP_TILES, :].rearrange("p m d -> p (m d)"), in_=v_sb[:]
            )

        idle = idle_psum.tile([P, P], F32)

        def keep_warm(count):
            for n in range(count):
                nc.tensor.matmul(idle[:], ident[:], ident[:], start=True, stop=True)

        vec = nc.vector.tensor_copy
        sca = nc.scalar.copy

        turn_x(0)
        keep_warm(3)
        regroup(vec, chunks[0], 0, 0, 256)
        copy_x(0)
        quantise_x(0)
        regroup(sca, chunks[0], 1, 128, 256)
        regroup(vec, chunks[0], 1, 0, 128)
        quantise_weights(chunks[0], 0, 1)
        quantise_weights(chunks[0], 1, 2)
        turn_x(1)
        keep_warm(1)
        copy_x(1)
        multiply_q(0, 0)
        turn_x(2)
        copy_x(2)
        rotate_q(0, 0)
        quantise_x(1)
        for m in range(1, TILES):
            if m + 2 < TILES:
                turn_x(m + 2)
                keep_warm(m % 2)
                copy_x(m + 2)
                if m + 2 in (3, 4, 5, 6):
                    at = (3, 4, 5, 6).index(m + 2)
                    regroup(sca, chunks[1], at // 2, 128 * (at % 2), 128 * (at % 2) + 128)
            multiply_q(0, m)
            if m + 1 < TILES:
                quantise_x(m + 1)
            if m == TILES - 1:
                quantise_weights(chunks[1], 0, 2)
            rotate_q(0, m)
            if m in (2, 4, 6):
                finish_first(0, m - 2, nc.vector)
        finish_first(0, 6, nc.gpsimd)
        for g in range(PASSES):
            for w in range(2):
                regroup(sca, kv, g, HD * w, HD * (w + 1))
        for g in range(PASSES):
            for h in range(2):
                regroup(sca, chunks[2], g, 256 * h, 256 * (h + 1))
        for m in range(TILES):
            multiply_q(1, m)
            if m == 4:
                quantise_weights(kv, 0, 2)
            rotate_q(1, m)
            if m % 2 == 1:
                finish_first(1, m - 1, nc.gpsimd)
        for w in range(2):
            for first in range(0, TILES, GROUP_TILES):
                multiply_kv(w, first)
        for first in range(0, TILES, GROUP_TILES):
            store_v(first)
        rotate_k(0)
        quantise_weights(chunks[2], 0, 2)
        rotate_k(GROUP_TILES)
        for first in range(0, TILES, GROUP_TILES):
            finish_k(nc.gpsimd, first)
        for m in range(TILES):
            multiply_q(2, m)
            rotate_q(2, m)
            if m < 6:
                finish_q(nc.gpsimd, 2, m)
        for m in range(6, TILES):
            finish_q(nc.vector, 2, m)
